import numpy as np
import ml_dtypes


def mxq(x, axis, fmt="e4m3"):
    dtype, down = {"e4m3": (ml_dtypes.float8_e4m3fn, 7), "e5m2": (ml_dtypes.float8_e5m2, 14)}[fmt]
    v = np.moveaxis(np.asarray(x, np.float32).astype(ml_dtypes.bfloat16).astype(np.float64), axis, -1)
    blocks = v.reshape(v.shape[:-1] + (-1, 32))
    amax = np.abs(blocks).max(-1, keepdims=True)
    byte = np.maximum(np.where(amax > 0, np.frexp(amax)[1] - 1 + 127, 0) - down, 1)
    scale = np.exp2(byte - 127.0)
    codes = (blocks / scale).astype(np.float32).astype(dtype).astype(np.float64)
    return np.moveaxis((codes * scale).reshape(v.shape), -1, axis)


WIDE = False


def mx_kscale(k):
    if not WIDE:
        return np.ones(k)
    levels = np.array([10, -10, 5, -5, 0])
    if k % 512:
        return np.exp2(np.random.permutation(np.resize(levels, k // 32))).repeat(32)
    a = np.empty((k // 512, 16))
    for p in range(k // 512):
        a[p, :8] = np.random.permutation(np.resize(levels, 8))
        for g in range(8):
            far = levels[np.abs(levels - a[p, g]) >= 10]
            a[p, g + 8] = far[np.random.randint(len(far))]
    return np.exp2(a.ravel()).repeat(32)


BF16 = ml_dtypes.bfloat16


def bf(x):
    return np.asarray(x, np.float32).astype(BF16)


def f64(x):
    return np.asarray(x).astype(np.float64)


S, E, C, HD, HP = 2048, 768, 256, 1024, 1024
R = 2 * HP


def sigmoid(v):
    return 1.0 / (1.0 + np.exp(-v))


def draw0():
    s, t = mx_kscale(R), mx_kscale(HD)
    return {"r": bf(np.abs(np.random.standard_normal((C, R))) * 0.5 * s),
            "psi_w1": bf(np.random.standard_normal((HD, R)) * 2.0 / np.sqrt(R) / s * t[:, None]),
            "psi_b1": bf(np.random.standard_normal(HD) * 0.3 * t),
            "w_dw": bf(np.random.standard_normal((E, HD)) * 1.5 / np.sqrt(HD) / t),
            "b_dw": bf(np.random.standard_normal(E) * 0.3),
            "w_gate": bf(np.random.standard_normal((E, HD)) * 1.5 / np.sqrt(HD) / t),
            "b_gate": bf(np.random.standard_normal(E) * 0.3),
            "W0": bf(np.random.standard_normal(E) * 0.1)}


def core(r, psi_w1, psi_b1, w_dw, b_dw, w_gate, b_gate, W0):
    hid = np.maximum((mxq(f64(r), 1, "e4m3") @ mxq(f64(psi_w1), 1, "e4m3").T) + f64(psi_b1), 0.0)
    hq = mxq(hid, 1, "e4m3")
    dW = (hq @ mxq(f64(w_dw), 1, "e4m3").T) + f64(b_dw)
    gate = sigmoid((hq @ mxq(f64(w_gate), 1, "e4m3").T) + f64(b_gate))
    return f64(W0)[None, :] + gate * dW


def e4m3fn_bytes(y):
    return np.clip(np.asarray(y, np.float64), -448.0, 448.0).astype(np.float32).astype(ml_dtypes.float8_e4m3fn).view(np.uint8)


def e4m3fn_values(b):
    return np.asarray(b, np.uint8).view(ml_dtypes.float8_e4m3fn).astype(np.float64)


def setup_inputs():
    d = draw0()
    x0 = np.asarray(d['w_gate']).astype(np.float64)
    s = (np.max(np.abs(x0), axis=(0,), keepdims=True) / 448.0).astype(np.float32)
    out = {}
    for k, v in d.items():
        if k == 'w_gate':
            out['w_gate_bytes'] = e4m3fn_bytes(x0 / s.astype(np.float64))
            out['w_gate_scale'] = s
        else:
            out[k] = v
    return out


def reference(r, psi_w1, psi_b1, w_dw, b_dw, w_gate_bytes, w_gate_scale, b_gate, W0):
    return core(r, psi_w1, psi_b1, w_dw, b_dw, e4m3fn_values(w_gate_bytes) * w_gate_scale.astype(np.float64), b_gate, W0)

@@ -1,0 +1,262 @@
+from contextlib import ExitStack
+
+import concourse.mybir as mybir
+from concourse.masks import make_identity
+
+C, R, HD, E = 256, 2048, 1024, 768
+FLOPS = 2 * C * (R * HD + HD * 2 * E)
+
+F32 = mybir.dt.float32
+BF16 = mybir.dt.bfloat16
+U32 = mybir.dt.uint32
+U8 = mybir.dt.uint8
+FP8 = mybir.dt.float8_e4m3fn
+FP8X4 = mybir.dt.float8_e4m3fn_x4
+ACT = mybir.ActivationFunctionType
+ALU = mybir.AluOpType
+
+P = 128
+BANK = 512
+R_STEPS = 2
+PSI_STEPS = 8
+W_STEPS = 6
+E_PAIRS = 3
+FIRST_PSI = R_STEPS
+FIRST_W = R_STEPS + PSI_STEPS
+STEPS = FIRST_W + W_STEPS
+HID_LAG = 2
+OUT_LAG = 3
+
+
+def tile_metalinearheadml_pb_kernel(
+    tc, r, psi_w1, psi_b1, w_dw, b_dw, w_gate_bytes, w_gate_scale, b_gate, W0, out
+):
+    nc = tc.nc
+    with ExitStack() as ctx:
+        keep = ctx.enter_context(tc.tile_pool(name="keep", bufs=1))
+        ring = ctx.enter_context(tc.tile_pool(name="ring", bufs=4))
+        psum = ctx.enter_context(tc.psum_pool(name="psum", bufs=8))
+        ctx.enter_context(tc.manual_schedule())
+
+        def new_bank():
+            return psum.tile([P, BANK], F32, name="bank", tag="bank")
+
+        ident = keep.tile([P, P], F32, name="ident")
+        make_identity(nc, ident[:])
+
+        scale_cols = keep.tile([P, 8], F32, name="scale_cols")
+        nc.scalar.dma_start(out=scale_cols[:], in_=w_gate_scale.rearrange("o (p i) -> p (o i)", i=8))
+
+        r_sb = {}
+        for b in range(R_STEPS):
+            for h in range(2):
+                r_sb[b, h] = keep.tile([P, 1024], BF16, name="r_%d_%d" % (b, h), align_bytes=256)
+                nc.sync.dma_start(out=r_sb[b, h][:], in_=r[P * h : P * (h + 1), 1024 * b : 1024 * (b + 1)])
+
+        psi_rows = psi_w1.rearrange("(g p t) k -> g t p k", p=P, t=4)
+        gate_rows = w_gate_bytes.rearrange("(a p j) k -> a p (j k)", p=P, j=2)
+        dw_rows = w_dw.rearrange("(a p j) k -> a p (j k)", p=P, j=2)
+        psi_sb, gate_bytes, dw_sb = [], [], []
+        b1_raw = keep.tile([P, 2, 4], BF16, name="b1_raw")
+        bd_raw = keep.tile([P, E_PAIRS, 2], BF16, name="bd_raw")
+        bg_raw = keep.tile([P, E_PAIRS, 2], BF16, name="bg_raw")
+        w0_rows = keep.tile([P, E], BF16, name="w0_rows")
+        for i in range(PSI_STEPS):
+            psi_sb.append(keep.tile([P, R], BF16, name="psi_%d" % i, align_bytes=256))
+            nc.sync.dma_start(out=psi_sb[i][:], in_=psi_rows[i // 4, i % 4])
+            if i == 1:
+                nc.sync.dma_start(out=b1_raw[:], in_=psi_b1.rearrange("(g p t) -> p g t", p=P, t=4))
+            if 3 <= i < 3 + E_PAIRS:
+                a = i - 3
+                gate_bytes.append(keep.tile([P, 2 * HD], U8, name="gate_bytes_%d" % a, align_bytes=256))
+                nc.sync.dma_start(out=gate_bytes[a][:], in_=gate_rows[a])
+        for a in range(E_PAIRS):
+            dw_sb.append(keep.tile([P, 2 * HD], BF16, name="dw_%d" % a, align_bytes=256))
+            nc.sync.dma_start(out=dw_sb[a][:], in_=dw_rows[a])
+        nc.sync.dma_start(out=bd_raw[:], in_=b_dw.rearrange("(a p j) -> p a j", p=P, j=2))
+        nc.sync.dma_start(out=bg_raw[:], in_=b_gate.rearrange("(a p j) -> p a j", p=P, j=2))
+        nc.sync.dma_start(out=w0_rows[:], in_=W0.partition_broadcast(P))
+
+        scale_rows = keep.tile([P, HD], F32, name="scale_rows")
+        for u in range(2):
+            bank = new_bank()
+            for h in range(2):
+                for e in range(2):
+                    i = 4 * h + 2 * u + e
+                    nc.tensor.transpose(
+                        bank[:, P * (2 * h + e) : P * (2 * h + e + 1)],
+                        scale_cols[:, i : i + 1].to_broadcast([P, P]),
+                        ident[:],
+                    )
+            nc.scalar.activation(
+                out=scale_rows[:, BANK * u : BANK * (u + 1)].rearrange("n (p h e) -> n p h e", h=2, e=2),
+                in_=bank[:].rearrange("n (h e p) -> n p h e", h=2, e=2),
+                func=ACT.Copy,
+            )
+
+        b1 = keep.tile([P, 2, 4], F32, name="b1")
+        bd = keep.tile([P, E_PAIRS, 2], F32, name="bd")
+        bg = keep.tile([P, E_PAIRS, 2], F32, name="bg")
+
+        gate_wide = {}
+        codes, scales = {}, {}
+        hid_planes, hid_codes, hid_scales = {}, {}, {}
+        prod = {}
+
+        def every_second_word(words, g, u):
+            return words[:, 256 * g + u : 256 * (g + 1) : 2]
+
+        def step_sources(s, half):
+            gu = [(g, u) for g in range(2) for u in range(2)]
+            if s < FIRST_PSI:
+                words = r_sb[s, half][:].bitcast(F32)
+                return [every_second_word(words, g, u) for g, u in gu]
+            if s < FIRST_W:
+                words = psi_sb[s - FIRST_PSI][:].bitcast(F32)
+                return [every_second_word(words, 2 * half + g, u) for g, u in gu]
+            n = s - FIRST_W
+            if half == 0:
+                words = dw_sb[n // 2][:].bitcast(F32)
+                return [every_second_word(words, 2 * (n % 2) + g, u) for g, u in gu]
+            words = gate_wide[n][:].bitcast(F32)
+            return [words[:, 256 * u + P * g : 256 * u + P * (g + 1)] for g, u in gu]
+
+        def transpose_step(s):
+            grouped = ring.tile([P, 2048], BF16, name="grouped", tag="grouped", align_bytes=64)
+            for half in range(2):
+                bank = new_bank()
+                for i, src in enumerate(step_sources(s, half)):
+                    nc.tensor.transpose(bank[:, P * i : P * (i + 1)], src, ident[:])
+                if s < FIRST_PSI:
+                    dst = grouped[:].bitcast(F32).rearrange("p (g h m u) -> p h g m u", g=2, h=2, u=2)
+                else:
+                    dst = grouped[:].bitcast(F32).rearrange("p (h g m u) -> p h g m u", g=2, h=2, u=2)
+                nc.scalar.copy(out=dst[:, half], in_=bank[:].rearrange("p (g u m) -> p g m u", g=2, u=2))
+            return grouped
+
+        def quantize_step(s, grouped):
+            codes[s] = keep.tile([P, 512], U32, name="codes_%d" % s, align_bytes=64)
+            scales[s] = keep.tile([P, 512], U8, name="scales_%d" % s, align_bytes=64)
+            nc.vector.quantize_mx(out=codes[s][:].bitcast(FP8X4), scales=scales[s][:], in_=grouped[:])
+
+        def widen_gate(n):
+            gate_wide[n] = keep.tile([P, HD], BF16, name="gate_wide_%d" % n)
+            j = n % 2
+            nc.vector.tensor_tensor(
+                out=gate_wide[n][:].rearrange("p (u q e) -> p u q e", u=2, e=2),
+                in0=gate_bytes[n // 2][:, HD * j : HD * (j + 1)].bitcast(FP8).rearrange("p (q u e) -> p u q e", u=2, e=2),
+                in1=scale_rows[:].rearrange("p (u q e) -> p u q e", u=2, e=2),
+                op=ALU.mult,
+            )
+
+        def hidden_tile(i):
+            g, t = divmod(i, 4)
+            s = FIRST_PSI + i
+            acc = new_bank()
+            for c in range(4):
+                cols = slice(P * c, P * (c + 1))
+                r_cols = slice(C * (c % 2), C * (c % 2 + 1))
+                nc.tensor.matmul_mx(
+                    out=acc[:, 0:C],
+                    lhsT=codes[s][:, cols].bitcast(FP8X4),
+                    lhsT_scale=scales[s][:, cols],
+                    rhs=codes[c // 2][:, r_cols].bitcast(FP8X4),
+                    rhs_scale=scales[c // 2][:, r_cols],
+                    start=(c == 0),
+                    stop=(c == 3),
+                )
+            if t == 0:
+                hid_planes[g] = keep.tile([P, 4, C], BF16, name="hid_planes_%d" % g)
+            nc.scalar.activation(
+                out=hid_planes[g][:, t, :], in_=acc[:, 0:C], func=ACT.Relu, bias=b1[:, g, t : t + 1]
+            )
+
+        def quantize_hidden(g):
+            hid_grouped = keep.tile([P, C, 4], BF16, name="hid_grouped_%d" % g, align_bytes=64)
+            nc.vector.tensor_copy(out=hid_grouped[:], in_=hid_planes[g][:].rearrange("p t c -> p c t"))
+            hid_codes[g] = keep.tile([P, C], U32, name="hid_codes_%d" % g, align_bytes=64)
+            hid_scales[g] = keep.tile([P, C], U8, name="hid_scales_%d" % g, align_bytes=64)
+            nc.vector.quantize_mx(
+                out=hid_codes[g][:].bitcast(FP8X4),
+                scales=hid_scales[g][:],
+                in_=hid_grouped[:].rearrange("p c t -> p (c t)"),
+            )
+
+        def second_product(n, which):
+            s = FIRST_W + n
+            acc = new_bank()
+            for g in range(2):
+                cols = slice(256 * which + P * g, 256 * which + P * (g + 1))
+                nc.tensor.matmul_mx(
+                    out=acc[:, 0:C],
+                    lhsT=codes[s][:, cols].bitcast(FP8X4),
+                    lhsT_scale=scales[s][:, cols],
+                    rhs=hid_codes[g][:].bitcast(FP8X4),
+                    rhs_scale=hid_scales[g][:],
+                    start=(g == 0),
+                    stop=(g == 1),
+                )
+            return acc
+
+        def gated_tile(n):
+            a, j = divmod(n, 2)
+            gate_acc = second_product(n, 1)
+            dw_acc = second_product(n, 0)
+            gate = ring.tile([P, C], F32, name="gate", tag="gate")
+            nc.scalar.activation(out=gate[:], in_=gate_acc[:, 0:C], func=ACT.Sigmoid, bias=bg[:, a, j : j + 1])
+            prod[n] = keep.tile([P, C], F32, name="prod_%d" % n)
+            nc.vector.scalar_tensor_tensor(
+                out=prod[n][:], in0=dw_acc[:, 0:C], scalar=bd[:, a, j : j + 1], in1=gate[:],
+                op0=ALU.add, op1=ALU.mult,
+            )
+
+        def turn_back(a):
+            bank = new_bank()
+            for h in range(2):
+                for j in range(2):
+                    nc.tensor.transpose(
+                        bank[:, P * (2 * h + j) : P * (2 * h + j + 1)],
+                        prod[2 * a + j][:, P * h : P * (h + 1)],
+                        ident[:],
+                    )
+            return bank
+
+        def add_and_store(a, bank):
+            e_cols = slice(256 * a, 256 * (a + 1))
+            for h in range(2):
+                result = ring.tile([P, 256], F32, name="result", tag="result")
+                nc.vector.tensor_tensor(
+                    out=result[:].rearrange("c (p j) -> c p j", j=2),
+                    in0=bank[:, 256 * h : 256 * (h + 1)].rearrange("c (j p) -> c p j", j=2),
+                    in1=w0_rows[:, e_cols].rearrange("c (p j) -> c p j", j=2),
+                    op=ALU.add,
+                )
+                nc.sync.dma_start(out=out[P * h : P * (h + 1), e_cols], in_=result[:])
+
+        hid_steps = [FIRST_PSI + 4 * g + 3 + HID_LAG for g in range(2)]
+        widen_steps = [s for s in range(5, STEPS) if s not in hid_steps][:W_STEPS]
+
+        for s in range(STEPS):
+            grouped = transpose_step(s)
+            if s == STEPS - 1:
+                first_bank = turn_back(0)
+            quantize_step(s, grouped)
+            if s == FIRST_PSI + 1:
+                nc.vector.tensor_copy(out=b1[:], in_=b1_raw[:])
+            if s == FIRST_W + 1:
+                nc.vector.tensor_copy(out=bd[:], in_=bd_raw[:])
+                nc.vector.tensor_copy(out=bg[:], in_=bg_raw[:])
+            if s == STEPS - 1:
+                add_and_store(0, first_bank)
+            if 0 <= s - FIRST_PSI - HID_LAG < PSI_STEPS:
+                hidden_tile(s - FIRST_PSI - HID_LAG)
+            if s in hid_steps:
+                quantize_hidden(hid_steps.index(s))
+            if s in widen_steps:
+                widen_gate(widen_steps.index(s))
+            if s - FIRST_W - OUT_LAG >= 0:
+                gated_tile(s - FIRST_W - OUT_LAG)
+        for n in range(W_STEPS - OUT_LAG, W_STEPS):
+            gated_tile(n)
+        for a in range(1, E_PAIRS):
+            add_and_store(a, turn_back(a))

@@ -17,15 +17,11 @@ ALU = mybir.AluOpType
 
 P = 128
 BANK = 512
-R_STEPS = 2
-PSI_STEPS = 8
-W_STEPS = 6
-E_PAIRS = 3
-FIRST_PSI = R_STEPS
-FIRST_W = R_STEPS + PSI_STEPS
-STEPS = FIRST_W + W_STEPS
-HID_LAG = 2
-OUT_LAG = 3
+HID_TILES = HD // P
+OUT_TILES = E // P
+OUT_PAIRS = OUT_TILES // 2
+GATE, DW = 0, 1
+PASS_HALVES = [(g, u) for g in range(2) for u in range(2)]
 
 
 def tile_metalinearheadml_pb_kernel(
@@ -35,11 +31,8 @@ def tile_metalinearheadml_pb_kernel(
     with ExitStack() as ctx:
         keep = ctx.enter_context(tc.tile_pool(name="keep", bufs=1))
         ring = ctx.enter_context(tc.tile_pool(name="ring", bufs=4))
-        psum = ctx.enter_context(tc.psum_pool(name="psum", bufs=8))
+        psum = ctx.enter_context(tc.psum_pool(name="psum", bufs=4))
         ctx.enter_context(tc.manual_schedule())
-
-        def new_bank():
-            return psum.tile([P, BANK], F32, name="bank", tag="bank")
 
         ident = keep.tile([P, P], F32, name="ident")
         make_identity(nc, ident[:])
@@ -47,8 +40,13 @@ def tile_metalinearheadml_pb_kernel(
         scale_cols = keep.tile([P, 8], F32, name="scale_cols")
         nc.scalar.dma_start(out=scale_cols[:], in_=w_gate_scale.rearrange("o (p i) -> p (o i)", i=8))
 
+        warm_in = keep.tile([P, 1], F32, name="warm_in")
+        warm_out = keep.tile([P, 1], F32, name="warm_out")
+        nc.vector.memset(warm_in[:], 0.0)
+        nc.scalar.activation(out=warm_out[:], in_=warm_in[:], func=ACT.Sigmoid)
+
         r_sb = {}
-        for b in range(R_STEPS):
+        for b in range(2):
             for h in range(2):
                 r_sb[b, h] = keep.tile([P, 1024], BF16, name="r_%d_%d" % (b, h), align_bytes=256)
                 nc.sync.dma_start(out=r_sb[b, h][:], in_=r[P * h : P * (h + 1), 1024 * b : 1024 * (b + 1)])
@@ -58,28 +56,32 @@ def tile_metalinearheadml_pb_kernel(
         dw_rows = w_dw.rearrange("(a p j) k -> a p (j k)", p=P, j=2)
         psi_sb, gate_bytes, dw_sb = [], [], []
         b1_raw = keep.tile([P, 2, 4], BF16, name="b1_raw")
-        bd_raw = keep.tile([P, E_PAIRS, 2], BF16, name="bd_raw")
-        bg_raw = keep.tile([P, E_PAIRS, 2], BF16, name="bg_raw")
-        w0_rows = keep.tile([P, E], BF16, name="w0_rows")
-        for i in range(PSI_STEPS):
+        for i in range(HID_TILES):
             psi_sb.append(keep.tile([P, R], BF16, name="psi_%d" % i, align_bytes=256))
             nc.sync.dma_start(out=psi_sb[i][:], in_=psi_rows[i // 4, i % 4])
             if i == 1:
                 nc.sync.dma_start(out=b1_raw[:], in_=psi_b1.rearrange("(g p t) -> p g t", p=P, t=4))
-            if 3 <= i < 3 + E_PAIRS:
-                a = i - 3
+            if 2 <= i < 2 + OUT_PAIRS:
+                a = i - 2
                 gate_bytes.append(keep.tile([P, 2 * HD], U8, name="gate_bytes_%d" % a, align_bytes=256))
                 nc.sync.dma_start(out=gate_bytes[a][:], in_=gate_rows[a])
-        for a in range(E_PAIRS):
+        for a in range(OUT_PAIRS):
             dw_sb.append(keep.tile([P, 2 * HD], BF16, name="dw_%d" % a, align_bytes=256))
             nc.sync.dma_start(out=dw_sb[a][:], in_=dw_rows[a])
-        nc.sync.dma_start(out=bd_raw[:], in_=b_dw.rearrange("(a p j) -> p a j", p=P, j=2))
-        nc.sync.dma_start(out=bg_raw[:], in_=b_gate.rearrange("(a p j) -> p a j", p=P, j=2))
+        bias_raw = {}
+        for which, vec in ((GATE, b_gate), (DW, b_dw)):
+            bias_raw[which] = keep.tile([P, OUT_PAIRS, 2], BF16, name="bias_raw_%d" % which)
+            nc.sync.dma_start(out=bias_raw[which][:], in_=vec.rearrange("(a p j) -> p a j", p=P, j=2))
+        w0_rows = keep.tile([P, E], BF16, name="w0_rows")
         nc.sync.dma_start(out=w0_rows[:], in_=W0.partition_broadcast(P))
 
         scale_rows = keep.tile([P, HD], F32, name="scale_rows")
-        for u in range(2):
-            bank = new_bank()
+        b1 = keep.tile([P, 2, 4], F32, name="b1")
+        bias, sorted_words, grouped, codes, scales = {}, {}, {}, {}, {}
+        hid_planes, accs, prod = {}, {}, {}
+
+        def spread_scale(u):
+            bank = psum.tile([P, BANK], F32, name="turn", tag="turn")
             for h in range(2):
                 for e in range(2):
                     i = 4 * h + 2 * u + e
@@ -88,140 +90,131 @@ def tile_metalinearheadml_pb_kernel(
                         scale_cols[:, i : i + 1].to_broadcast([P, P]),
                         ident[:],
                     )
-            nc.scalar.activation(
+            nc.vector.tensor_copy(
                 out=scale_rows[:, BANK * u : BANK * (u + 1)].rearrange("n (p h e) -> n p h e", h=2, e=2),
                 in_=bank[:].rearrange("n (h e p) -> n p h e", h=2, e=2),
-                func=ACT.Copy,
             )
 
-        b1 = keep.tile([P, 2, 4], F32, name="b1")
-        bd = keep.tile([P, E_PAIRS, 2], F32, name="bd")
-        bg = keep.tile([P, E_PAIRS, 2], F32, name="bg")
+        def turn(sources, dst):
+            bank = psum.tile([P, BANK], F32, name="turn", tag="turn")
+            for i, src in enumerate(sources):
+                nc.tensor.transpose(bank[:, P * i : P * (i + 1)], src, ident[:])
+            nc.scalar.copy(out=dst, in_=bank[:].rearrange("p (g u m) -> p g m u", g=2, u=2))
 
-        gate_wide = {}
-        codes, scales = {}, {}
-        hid_planes, hid_codes, hid_scales = {}, {}, {}
-        prod = {}
+        def every_second_word(words):
+            return [words[:, 256 * g + u : 256 * (g + 1) : 2] for g, u in PASS_HALVES]
 
-        def every_second_word(words, g, u):
-            return words[:, 256 * g + u : 256 * (g + 1) : 2]
+        def turn_r(b):
+            grouped["r", b] = ring.tile([P, 2048], BF16, name="grouped", tag="grouped", align_bytes=64)
+            dst = grouped["r", b][:].bitcast(F32).rearrange("p (g h m u) -> p h g m u", g=2, h=2, u=2)
+            for h in range(2):
+                turn(every_second_word(r_sb[b, h][:].bitcast(F32)), dst[:, h])
 
-        def step_sources(s, half):
-            gu = [(g, u) for g in range(2) for u in range(2)]
-            if s < FIRST_PSI:
-                words = r_sb[s, half][:].bitcast(F32)
-                return [every_second_word(words, g, u) for g, u in gu]
-            if s < FIRST_W:
-                words = psi_sb[s - FIRST_PSI][:].bitcast(F32)
-                return [every_second_word(words, 2 * half + g, u) for g, u in gu]
-            n = s - FIRST_W
-            if half == 0:
-                words = dw_sb[n // 2][:].bitcast(F32)
-                return [every_second_word(words, 2 * (n % 2) + g, u) for g, u in gu]
-            words = gate_wide[n][:].bitcast(F32)
-            return [words[:, 256 * u + P * g : 256 * u + P * (g + 1)] for g, u in gu]
+        def turn_psi(i):
+            grouped["psi", i] = ring.tile([P, 2048], BF16, name="grouped", tag="grouped", align_bytes=64)
+            dst = grouped["psi", i][:].bitcast(F32).rearrange("p (b g m u) -> p b g m u", b=2, g=2, u=2)
+            words = psi_sb[i][:].bitcast(F32)
+            for b in range(2):
+                turn(every_second_word(words[:, BANK * b : BANK * (b + 1)]), dst[:, b])
 
-        def transpose_step(s):
-            grouped = ring.tile([P, 2048], BF16, name="grouped", tag="grouped", align_bytes=64)
-            for half in range(2):
-                bank = new_bank()
-                for i, src in enumerate(step_sources(s, half)):
-                    nc.tensor.transpose(bank[:, P * i : P * (i + 1)], src, ident[:])
-                if s < FIRST_PSI:
-                    dst = grouped[:].bitcast(F32).rearrange("p (g h m u) -> p h g m u", g=2, h=2, u=2)
-                else:
-                    dst = grouped[:].bitcast(F32).rearrange("p (h g m u) -> p h g m u", g=2, h=2, u=2)
-                nc.scalar.copy(out=dst[:, half], in_=bank[:].rearrange("p (g u m) -> p g m u", g=2, u=2))
-            return grouped
+        def turn_weights(n):
+            for which in (GATE, DW):
+                grouped[which, n] = ring.tile([P, HD], BF16, name="grouped_w", tag="grouped_w", align_bytes=64)
+                words = sorted_words[which, n][:].bitcast(F32)
+                turn(
+                    [words[:, 256 * u + P * g : 256 * u + P * (g + 1)] for g, u in PASS_HALVES],
+                    grouped[which, n][:].bitcast(F32).rearrange("p (g m u) -> p g m u", g=2, u=2),
+                )
 
-        def quantize_step(s, grouped):
-            codes[s] = keep.tile([P, 512], U32, name="codes_%d" % s, align_bytes=64)
-            scales[s] = keep.tile([P, 512], U8, name="scales_%d" % s, align_bytes=64)
-            nc.vector.quantize_mx(out=codes[s][:].bitcast(FP8X4), scales=scales[s][:], in_=grouped[:])
+        def quantize(key):
+            width = grouped[key].shape[1] // 4
+            codes[key] = keep.tile([P, width], U32, name="codes_%s_%d" % key, align_bytes=64)
+            scales[key] = keep.tile([P, width], U8, name="scales_%s_%d" % key, align_bytes=64)
+            nc.vector.quantize_mx(out=codes[key][:].bitcast(FP8X4), scales=scales[key][:], in_=grouped[key][:])
+
+        def quantize_weights(n):
+            quantize((GATE, n))
+            quantize((DW, n))
 
         def widen_gate(n):
-            gate_wide[n] = keep.tile([P, HD], BF16, name="gate_wide_%d" % n)
-            j = n % 2
+            a, j = divmod(n, 2)
+            sorted_words[GATE, n] = keep.tile([P, HD], BF16, name="gate_wide_%d" % n)
             nc.vector.tensor_tensor(
-                out=gate_wide[n][:].rearrange("p (u q e) -> p u q e", u=2, e=2),
-                in0=gate_bytes[n // 2][:, HD * j : HD * (j + 1)].bitcast(FP8).rearrange("p (q u e) -> p u q e", u=2, e=2),
+                out=sorted_words[GATE, n][:].rearrange("p (u q e) -> p u q e", u=2, e=2),
+                in0=gate_bytes[a][:, HD * j : HD * (j + 1)].bitcast(FP8).rearrange("p (q u e) -> p u q e", u=2, e=2),
                 in1=scale_rows[:].rearrange("p (u q e) -> p u q e", u=2, e=2),
                 op=ALU.mult,
             )
 
+        def sort_dw(n):
+            a, j = divmod(n, 2)
+            sorted_words[DW, n] = keep.tile([P, HD], BF16, name="dw_sorted_%d" % n)
+            nc.vector.tensor_copy(
+                out=sorted_words[DW, n][:].bitcast(F32).rearrange("p (u q) -> p u q", u=2),
+                in_=dw_sb[a][:, HD * j : HD * (j + 1)].bitcast(F32).rearrange("p (q u) -> p u q", u=2),
+            )
+
+        def mx_pass(acc, lhs_key, lhs_cols, rhs_key, rhs_cols, start, stop):
+            nc.tensor.matmul_mx(
+                out=acc[:, 0:C],
+                lhsT=codes[lhs_key][:, lhs_cols].bitcast(FP8X4),
+                lhsT_scale=scales[lhs_key][:, lhs_cols],
+                rhs=codes[rhs_key][:, rhs_cols].bitcast(FP8X4),
+                rhs_scale=scales[rhs_key][:, rhs_cols],
+                start=start,
+                stop=stop,
+            )
+
         def hidden_tile(i):
             g, t = divmod(i, 4)
-            s = FIRST_PSI + i
-            acc = new_bank()
+            acc = psum.tile([P, BANK], F32, name="acc", tag="acc")
             for c in range(4):
-                cols = slice(P * c, P * (c + 1))
-                r_cols = slice(C * (c % 2), C * (c % 2 + 1))
-                nc.tensor.matmul_mx(
-                    out=acc[:, 0:C],
-                    lhsT=codes[s][:, cols].bitcast(FP8X4),
-                    lhsT_scale=scales[s][:, cols],
-                    rhs=codes[c // 2][:, r_cols].bitcast(FP8X4),
-                    rhs_scale=scales[c // 2][:, r_cols],
-                    start=(c == 0),
-                    stop=(c == 3),
-                )
+                b, half = divmod(c, 2)
+                mx_pass(acc, ("psi", i), slice(P * c, P * (c + 1)), ("r", b), slice(C * half, C * (half + 1)), c == 0, c == 3)
             if t == 0:
                 hid_planes[g] = keep.tile([P, 4, C], BF16, name="hid_planes_%d" % g)
-            nc.scalar.activation(
-                out=hid_planes[g][:, t, :], in_=acc[:, 0:C], func=ACT.Relu, bias=b1[:, g, t : t + 1]
-            )
+            nc.scalar.activation(out=hid_planes[g][:, t, :], in_=acc[:, 0:C], func=ACT.Relu, bias=b1[:, g, t : t + 1])
 
         def quantize_hidden(g):
-            hid_grouped = keep.tile([P, C, 4], BF16, name="hid_grouped_%d" % g, align_bytes=64)
-            nc.vector.tensor_copy(out=hid_grouped[:], in_=hid_planes[g][:].rearrange("p t c -> p c t"))
-            hid_codes[g] = keep.tile([P, C], U32, name="hid_codes_%d" % g, align_bytes=64)
-            hid_scales[g] = keep.tile([P, C], U8, name="hid_scales_%d" % g, align_bytes=64)
-            nc.vector.quantize_mx(
-                out=hid_codes[g][:].bitcast(FP8X4),
-                scales=hid_scales[g][:],
-                in_=hid_grouped[:].rearrange("p c t -> p (c t)"),
+            grouped["hid", g] = keep.tile([P, 4 * C], BF16, name="hid_grouped_%d" % g, align_bytes=64)
+            nc.vector.tensor_copy(
+                out=grouped["hid", g][:].rearrange("p (c t) -> p c t", t=4),
+                in_=hid_planes[g][:].rearrange("p t c -> p c t"),
             )
+            quantize(("hid", g))
 
-        def second_product(n, which):
-            s = FIRST_W + n
-            acc = new_bank()
-            for g in range(2):
-                cols = slice(256 * which + P * g, 256 * which + P * (g + 1))
-                nc.tensor.matmul_mx(
-                    out=acc[:, 0:C],
-                    lhsT=codes[s][:, cols].bitcast(FP8X4),
-                    lhsT_scale=scales[s][:, cols],
-                    rhs=hid_codes[g][:].bitcast(FP8X4),
-                    rhs_scale=hid_scales[g][:],
-                    start=(g == 0),
-                    stop=(g == 1),
-                )
-            return acc
+        def second_pass(n, which, g):
+            if g == 0:
+                accs[which, n] = psum.tile([P, BANK], F32, name="acc", tag="acc")
+            mx_pass(accs[which, n], (which, n), slice(P * g, P * (g + 1)), ("hid", g), slice(0, C), g == 0, g == 1)
 
-        def gated_tile(n):
+        def gate_product(n):
             a, j = divmod(n, 2)
-            gate_acc = second_product(n, 1)
-            dw_acc = second_product(n, 0)
             gate = ring.tile([P, C], F32, name="gate", tag="gate")
-            nc.scalar.activation(out=gate[:], in_=gate_acc[:, 0:C], func=ACT.Sigmoid, bias=bg[:, a, j : j + 1])
+            nc.scalar.activation(
+                out=gate[:], in_=accs[GATE, n][:, 0:C], func=ACT.Sigmoid, bias=bias[GATE][:, a, j : j + 1]
+            )
             prod[n] = keep.tile([P, C], F32, name="prod_%d" % n)
             nc.vector.scalar_tensor_tensor(
-                out=prod[n][:], in0=dw_acc[:, 0:C], scalar=bd[:, a, j : j + 1], in1=gate[:],
+                out=prod[n][:], in0=accs[DW, n][:, 0:C], scalar=bias[DW][:, a, j : j + 1], in1=gate[:],
                 op0=ALU.add, op1=ALU.mult,
             )
 
-        def turn_back(a):
-            bank = new_bank()
-            for h in range(2):
-                for j in range(2):
+        def out_tile(n):
+            for which in (GATE, DW):
+                for g in range(2):
+                    second_pass(n, which, g)
+            gate_product(n)
+
+        def store_pair(a):
+            bank = psum.tile([P, BANK], F32, name="turn", tag="turn")
+            for j in range(2):
+                for h in range(2):
                     nc.tensor.transpose(
                         bank[:, P * (2 * h + j) : P * (2 * h + j + 1)],
                         prod[2 * a + j][:, P * h : P * (h + 1)],
                         ident[:],
                     )
-            return bank
-
-        def add_and_store(a, bank):
             e_cols = slice(256 * a, 256 * (a + 1))
             for h in range(2):
                 result = ring.tile([P, 256], F32, name="result", tag="result")
@@ -233,30 +226,63 @@ def tile_metalinearheadml_pb_kernel(
                 )
                 nc.sync.dma_start(out=out[P * h : P * (h + 1), e_cols], in_=result[:])
 
-        hid_steps = [FIRST_PSI + 4 * g + 3 + HID_LAG for g in range(2)]
-        widen_steps = [s for s in range(5, STEPS) if s not in hid_steps][:W_STEPS]
-
-        for s in range(STEPS):
-            grouped = transpose_step(s)
-            if s == STEPS - 1:
-                first_bank = turn_back(0)
-            quantize_step(s, grouped)
-            if s == FIRST_PSI + 1:
-                nc.vector.tensor_copy(out=b1[:], in_=b1_raw[:])
-            if s == FIRST_W + 1:
-                nc.vector.tensor_copy(out=bd[:], in_=bd_raw[:])
-                nc.vector.tensor_copy(out=bg[:], in_=bg_raw[:])
-            if s == STEPS - 1:
-                add_and_store(0, first_bank)
-            if 0 <= s - FIRST_PSI - HID_LAG < PSI_STEPS:
-                hidden_tile(s - FIRST_PSI - HID_LAG)
-            if s in hid_steps:
-                quantize_hidden(hid_steps.index(s))
-            if s in widen_steps:
-                widen_gate(widen_steps.index(s))
-            if s - FIRST_W - OUT_LAG >= 0:
-                gated_tile(s - FIRST_W - OUT_LAG)
-        for n in range(W_STEPS - OUT_LAG, W_STEPS):
-            gated_tile(n)
-        for a in range(1, E_PAIRS):
-            add_and_store(a, turn_back(a))
+        spread_scale(0)
+        turn_r(0)
+        quantize(("r", 0))
+        turn_r(1)
+        spread_scale(1)
+        quantize(("r", 1))
+        turn_psi(0)
+        nc.vector.tensor_copy(out=b1[:], in_=b1_raw[:])
+        quantize(("psi", 0))
+        turn_psi(1)
+        widen_gate(0)
+        for i in range(2, 6):
+            turn_psi(i)
+            quantize(("psi", i - 1))
+            hidden_tile(i - 2)
+            widen_gate(i - 1)
+        turn_psi(6)
+        quantize(("psi", 5))
+        quantize_hidden(0)
+        sort_dw(0)
+        hidden_tile(4)
+        turn_psi(7)
+        quantize(("psi", 6))
+        hidden_tile(5)
+        sort_dw(1)
+        widen_gate(5)
+        turn_weights(0)
+        quantize(("psi", 7))
+        for which in (DW, GATE):
+            bias[which] = keep.tile([P, OUT_PAIRS, 2], F32, name="bias_%d" % which)
+            nc.vector.tensor_copy(out=bias[which][:], in_=bias_raw[which][:])
+        hidden_tile(6)
+        sort_dw(2)
+        sort_dw(3)
+        quantize_weights(0)
+        turn_weights(1)
+        quantize_weights(1)
+        hidden_tile(7)
+        quantize_hidden(1)
+        sort_dw(4)
+        for g in range(2):
+            turn_weights(2 + g)
+            quantize_weights(2 + g)
+            for n in range(2):
+                for which in (GATE, DW):
+                    second_pass(n, which, g)
+            if g == 0:
+                sort_dw(5)
+        gate_product(0)
+        gate_product(1)
+        turn_weights(4)
+        quantize_weights(4)
+        out_tile(2)
+        store_pair(0)
+        turn_weights(5)
+        quantize_weights(5)
+        for n in range(3, OUT_TILES):
+            out_tile(n)
+        store_pair(1)
+        store_pair(2)

@@ -31,7 +31,7 @@ def tile_metalinearheadml_pb_kernel(
     with ExitStack() as ctx:
         keep = ctx.enter_context(tc.tile_pool(name="keep", bufs=1))
         ring = ctx.enter_context(tc.tile_pool(name="ring", bufs=4))
-        psum = ctx.enter_context(tc.psum_pool(name="psum", bufs=4))
+        psum = ctx.enter_context(tc.psum_pool(name="psum", bufs=8))
         ctx.enter_context(tc.manual_schedule())
 
         ident = keep.tile([P, P], F32, name="ident")
@@ -59,12 +59,12 @@ def tile_metalinearheadml_pb_kernel(
         for i in range(HID_TILES):
             psi_sb.append(keep.tile([P, R], BF16, name="psi_%d" % i, align_bytes=256))
             nc.sync.dma_start(out=psi_sb[i][:], in_=psi_rows[i // 4, i % 4])
-            if i == 1:
-                nc.sync.dma_start(out=b1_raw[:], in_=psi_b1.rearrange("(g p t) -> p g t", p=P, t=4))
             if 2 <= i < 2 + OUT_PAIRS:
                 a = i - 2
                 gate_bytes.append(keep.tile([P, 2 * HD], U8, name="gate_bytes_%d" % a, align_bytes=256))
                 nc.sync.dma_start(out=gate_bytes[a][:], in_=gate_rows[a])
+            if i == 2:
+                nc.sync.dma_start(out=b1_raw[:], in_=psi_b1.rearrange("(g p t) -> p g t", p=P, t=4))
         for a in range(OUT_PAIRS):
             dw_sb.append(keep.tile([P, 2 * HD], BF16, name="dw_%d" % a, align_bytes=256))
             nc.sync.dma_start(out=dw_sb[a][:], in_=dw_rows[a])
@@ -81,7 +81,7 @@ def tile_metalinearheadml_pb_kernel(
         hid_planes, accs, prod = {}, {}, {}
 
         def spread_scale(u):
-            bank = psum.tile([P, BANK], F32, name="turn", tag="turn")
+            bank = psum.tile([P, BANK], F32, name="bank", tag="bank")
             for h in range(2):
                 for e in range(2):
                     i = 4 * h + 2 * u + e
@@ -96,7 +96,7 @@ def tile_metalinearheadml_pb_kernel(
             )
 
         def turn(sources, dst):
-            bank = psum.tile([P, BANK], F32, name="turn", tag="turn")
+            bank = psum.tile([P, BANK], F32, name="bank", tag="bank")
             for i, src in enumerate(sources):
                 nc.tensor.transpose(bank[:, P * i : P * (i + 1)], src, ident[:])
             nc.scalar.copy(out=dst, in_=bank[:].rearrange("p (g u m) -> p g m u", g=2, u=2))
@@ -120,9 +120,14 @@ def tile_metalinearheadml_pb_kernel(
         def turn_weights(n):
             for which in (GATE, DW):
                 grouped[which, n] = ring.tile([P, HD], BF16, name="grouped_w", tag="grouped_w", align_bytes=64)
-                words = sorted_words[which, n][:].bitcast(F32)
+                if (which, n) in sorted_words:
+                    words = sorted_words[which, n][:].bitcast(F32)
+                    sources = [words[:, 256 * u + P * g : 256 * u + P * (g + 1)] for g, u in PASS_HALVES]
+                else:
+                    a, j = divmod(n, 2)
+                    sources = every_second_word(dw_sb[a][:, HD * j : HD * (j + 1)].bitcast(F32))
                 turn(
-                    [words[:, 256 * u + P * g : 256 * u + P * (g + 1)] for g, u in PASS_HALVES],
+                    sources,
                     grouped[which, n][:].bitcast(F32).rearrange("p (g m u) -> p g m u", g=2, u=2),
                 )
 
@@ -167,7 +172,7 @@ def tile_metalinearheadml_pb_kernel(
 
         def hidden_tile(i):
             g, t = divmod(i, 4)
-            acc = psum.tile([P, BANK], F32, name="acc", tag="acc")
+            acc = psum.tile([P, BANK], F32, name="bank", tag="bank")
             for c in range(4):
                 b, half = divmod(c, 2)
                 mx_pass(acc, ("psi", i), slice(P * c, P * (c + 1)), ("r", b), slice(C * half, C * (half + 1)), c == 0, c == 3)
@@ -175,17 +180,16 @@ def tile_metalinearheadml_pb_kernel(
                 hid_planes[g] = keep.tile([P, 4, C], BF16, name="hid_planes_%d" % g)
             nc.scalar.activation(out=hid_planes[g][:, t, :], in_=acc[:, 0:C], func=ACT.Relu, bias=b1[:, g, t : t + 1])
 
-        def quantize_hidden(g):
+        def interleave_hidden(g):
             grouped["hid", g] = keep.tile([P, 4 * C], BF16, name="hid_grouped_%d" % g, align_bytes=64)
             nc.vector.tensor_copy(
                 out=grouped["hid", g][:].rearrange("p (c t) -> p c t", t=4),
                 in_=hid_planes[g][:].rearrange("p t c -> p c t"),
             )
-            quantize(("hid", g))
 
         def second_pass(n, which, g):
             if g == 0:
-                accs[which, n] = psum.tile([P, BANK], F32, name="acc", tag="acc")
+                accs[which, n] = psum.tile([P, BANK], F32, name="bank", tag="bank")
             mx_pass(accs[which, n], (which, n), slice(P * g, P * (g + 1)), ("hid", g), slice(0, C), g == 0, g == 1)
 
         def gate_product(n):
@@ -206,8 +210,8 @@ def tile_metalinearheadml_pb_kernel(
                     second_pass(n, which, g)
             gate_product(n)
 
-        def store_pair(a):
-            bank = psum.tile([P, BANK], F32, name="turn", tag="turn")
+        def turn_pair(a):
+            bank = psum.tile([P, BANK], F32, name="bank", tag="bank")
             for j in range(2):
                 for h in range(2):
                     nc.tensor.transpose(
@@ -215,6 +219,9 @@ def tile_metalinearheadml_pb_kernel(
                         prod[2 * a + j][:, P * h : P * (h + 1)],
                         ident[:],
                     )
+            return bank
+
+        def store_pair(a, bank):
             e_cols = slice(256 * a, 256 * (a + 1))
             for h in range(2):
                 result = ring.tile([P, 256], F32, name="result", tag="result")
@@ -233,39 +240,33 @@ def tile_metalinearheadml_pb_kernel(
         spread_scale(1)
         quantize(("r", 1))
         turn_psi(0)
-        nc.vector.tensor_copy(out=b1[:], in_=b1_raw[:])
         quantize(("psi", 0))
         turn_psi(1)
         widen_gate(0)
-        for i in range(2, 6):
+        for i in range(2, HID_TILES):
             turn_psi(i)
+            if i == 2:
+                nc.scalar.copy(out=b1[:], in_=b1_raw[:])
             quantize(("psi", i - 1))
             hidden_tile(i - 2)
-            widen_gate(i - 1)
-        turn_psi(6)
-        quantize(("psi", 5))
-        quantize_hidden(0)
-        sort_dw(0)
-        hidden_tile(4)
-        turn_psi(7)
-        quantize(("psi", 6))
-        hidden_tile(5)
-        sort_dw(1)
-        widen_gate(5)
+            if i < 6:
+                widen_gate(i - 1)
+            if i == 6:
+                interleave_hidden(0)
+                sort_dw(0)
+                quantize(("hid", 0))
+            if i == 7:
+                sort_dw(1)
+                widen_gate(5)
         turn_weights(0)
         quantize(("psi", 7))
-        for which in (DW, GATE):
-            bias[which] = keep.tile([P, OUT_PAIRS, 2], F32, name="bias_%d" % which)
-            nc.vector.tensor_copy(out=bias[which][:], in_=bias_raw[which][:])
         hidden_tile(6)
-        sort_dw(2)
-        sort_dw(3)
         quantize_weights(0)
         turn_weights(1)
         quantize_weights(1)
         hidden_tile(7)
-        quantize_hidden(1)
-        sort_dw(4)
+        interleave_hidden(1)
+        quantize(("hid", 1))
         for g in range(2):
             turn_weights(2 + g)
             quantize_weights(2 + g)
@@ -273,16 +274,20 @@ def tile_metalinearheadml_pb_kernel(
                 for which in (GATE, DW):
                     second_pass(n, which, g)
             if g == 0:
+                for which in (DW, GATE):
+                    bias[which] = keep.tile([P, OUT_PAIRS, 2], F32, name="bias_%d" % which)
+                    nc.scalar.copy(out=bias[which][:], in_=bias_raw[which][:])
+                sort_dw(4)
                 sort_dw(5)
         gate_product(0)
         gate_product(1)
         turn_weights(4)
-        quantize_weights(4)
-        out_tile(2)
-        store_pair(0)
         turn_weights(5)
+        first_pair = turn_pair(0)
+        quantize_weights(4)
+        store_pair(0, first_pair)
         quantize_weights(5)
-        for n in range(3, OUT_TILES):
+        for n in range(2, OUT_TILES):
             out_tile(n)
-        store_pair(1)
-        store_pair(2)
+        for a in range(1, OUT_PAIRS):
+            store_pair(a, turn_pair(a))

from contextlib import ExitStack

import concourse.mybir as mybir
from concourse.masks import make_identity

C, R, HD, E = 256, 2048, 1024, 768
FLOPS = 2 * C * (R * HD + HD * 2 * E)

F32 = mybir.dt.float32
BF16 = mybir.dt.bfloat16
U32 = mybir.dt.uint32
U8 = mybir.dt.uint8
FP8 = mybir.dt.float8_e4m3fn
FP8X4 = mybir.dt.float8_e4m3fn_x4
ACT = mybir.ActivationFunctionType
ALU = mybir.AluOpType

P = 128
BANK = 512
HID_TILES = HD // P
OUT_TILES = E // P
OUT_PAIRS = OUT_TILES // 2
GATE, DW = 0, 1
PASS_HALVES = [(g, u) for g in range(2) for u in range(2)]


def tile_metalinearheadml_pb_kernel(
    tc, r, psi_w1, psi_b1, w_dw, b_dw, w_gate_bytes, w_gate_scale, b_gate, W0, out
):
    nc = tc.nc
    with ExitStack() as ctx:
        keep = ctx.enter_context(tc.tile_pool(name="keep", bufs=1))
        ring = ctx.enter_context(tc.tile_pool(name="ring", bufs=4))
        psum = ctx.enter_context(tc.psum_pool(name="psum", bufs=8))
        ctx.enter_context(tc.manual_schedule())

        ident = keep.tile([P, P], F32, name="ident")
        make_identity(nc, ident[:])

        scale_cols = keep.tile([P, 8], F32, name="scale_cols")
        nc.scalar.dma_start(out=scale_cols[:], in_=w_gate_scale.rearrange("o (p i) -> p (o i)", i=8))

        warm_in = keep.tile([P, 1], F32, name="warm_in")
        warm_out = keep.tile([P, 1], F32, name="warm_out")
        nc.vector.memset(warm_in[:], 0.0)
        nc.scalar.activation(out=warm_out[:], in_=warm_in[:], func=ACT.Sigmoid)

        r_sb = {}
        for b in range(2):
            for h in range(2):
                r_sb[b, h] = keep.tile([P, 1024], BF16, name="r_%d_%d" % (b, h), align_bytes=256)
                nc.sync.dma_start(out=r_sb[b, h][:], in_=r[P * h : P * (h + 1), 1024 * b : 1024 * (b + 1)])

        psi_rows = psi_w1.rearrange("(g p t) k -> g t p k", p=P, t=4)
        gate_rows = w_gate_bytes.rearrange("(a p j) k -> a p (j k)", p=P, j=2)
        dw_rows = w_dw.rearrange("(a p j) k -> a p (j k)", p=P, j=2)
        psi_sb, gate_bytes, dw_sb = [], [], []
        b1_raw = keep.tile([P, 2, 4], BF16, name="b1_raw")
        for i in range(HID_TILES):
            psi_sb.append(keep.tile([P, R], BF16, name="psi_%d" % i, align_bytes=256))
            nc.sync.dma_start(out=psi_sb[i][:], in_=psi_rows[i // 4, i % 4])
            if 2 <= i < 2 + OUT_PAIRS:
                a = i - 2
                gate_bytes.append(keep.tile([P, 2 * HD], U8, name="gate_bytes_%d" % a, align_bytes=256))
                nc.sync.dma_start(out=gate_bytes[a][:], in_=gate_rows[a])
            if i == 2:
                nc.sync.dma_start(out=b1_raw[:], in_=psi_b1.rearrange("(g p t) -> p g t", p=P, t=4))
        for a in range(OUT_PAIRS):
            dw_sb.append(keep.tile([P, 2 * HD], BF16, name="dw_%d" % a, align_bytes=256))
            nc.sync.dma_start(out=dw_sb[a][:], in_=dw_rows[a])
        bias_raw = {}
        for which, vec in ((GATE, b_gate), (DW, b_dw)):
            bias_raw[which] = keep.tile([P, OUT_PAIRS, 2], BF16, name="bias_raw_%d" % which)
            nc.sync.dma_start(out=bias_raw[which][:], in_=vec.rearrange("(a p j) -> p a j", p=P, j=2))
        w0_rows = keep.tile([P, E], BF16, name="w0_rows")
        nc.sync.dma_start(out=w0_rows[:], in_=W0.partition_broadcast(P))

        scale_rows = keep.tile([P, HD], F32, name="scale_rows")
        b1 = keep.tile([P, 2, 4], F32, name="b1")
        bias, sorted_words, grouped, codes, scales = {}, {}, {}, {}, {}
        hid_planes, accs, prod = {}, {}, {}

        def spread_scale(u):
            bank = psum.tile([P, BANK], F32, name="bank", tag="bank")
            for h in range(2):
                for e in range(2):
                    i = 4 * h + 2 * u + e
                    nc.tensor.transpose(
                        bank[:, P * (2 * h + e) : P * (2 * h + e + 1)],
                        scale_cols[:, i : i + 1].to_broadcast([P, P]),
                        ident[:],
                    )
            nc.vector.tensor_copy(
                out=scale_rows[:, BANK * u : BANK * (u + 1)].rearrange("n (p h e) -> n p h e", h=2, e=2),
                in_=bank[:].rearrange("n (h e p) -> n p h e", h=2, e=2),
            )

        def turn(sources, dst):
            bank = psum.tile([P, BANK], F32, name="bank", tag="bank")
            for i, src in enumerate(sources):
                nc.tensor.transpose(bank[:, P * i : P * (i + 1)], src, ident[:])
            nc.scalar.copy(out=dst, in_=bank[:].rearrange("p (g u m) -> p g m u", g=2, u=2))

        def every_second_word(words):
            return [words[:, 256 * g + u : 256 * (g + 1) : 2] for g, u in PASS_HALVES]

        def turn_r(b):
            grouped["r", b] = ring.tile([P, 2048], BF16, name="grouped", tag="grouped", align_bytes=64)
            dst = grouped["r", b][:].bitcast(F32).rearrange("p (g h m u) -> p h g m u", g=2, h=2, u=2)
            for h in range(2):
                turn(every_second_word(r_sb[b, h][:].bitcast(F32)), dst[:, h])

        def turn_psi(i):
            grouped["psi", i] = ring.tile([P, 2048], BF16, name="grouped", tag="grouped", align_bytes=64)
            dst = grouped["psi", i][:].bitcast(F32).rearrange("p (b g m u) -> p b g m u", b=2, g=2, u=2)
            words = psi_sb[i][:].bitcast(F32)
            for b in range(2):
                turn(every_second_word(words[:, BANK * b : BANK * (b + 1)]), dst[:, b])

        def turn_weights(n):
            for which in (GATE, DW):
                grouped[which, n] = ring.tile([P, HD], BF16, name="grouped_w", tag="grouped_w", align_bytes=64)
                if (which, n) in sorted_words:
                    words = sorted_words[which, n][:].bitcast(F32)
                    sources = [words[:, 256 * u + P * g : 256 * u + P * (g + 1)] for g, u in PASS_HALVES]
                else:
                    a, j = divmod(n, 2)
                    sources = every_second_word(dw_sb[a][:, HD * j : HD * (j + 1)].bitcast(F32))
                turn(
                    sources,
                    grouped[which, n][:].bitcast(F32).rearrange("p (g m u) -> p g m u", g=2, u=2),
                )

        def quantize(key):
            width = grouped[key].shape[1] // 4
            codes[key] = keep.tile([P, width], U32, name="codes_%s_%d" % key, align_bytes=64)
            scales[key] = keep.tile([P, width], U8, name="scales_%s_%d" % key, align_bytes=64)
            nc.vector.quantize_mx(out=codes[key][:].bitcast(FP8X4), scales=scales[key][:], in_=grouped[key][:])

        def quantize_weights(n):
            quantize((GATE, n))
            quantize((DW, n))

        def widen_gate(n):
            a, j = divmod(n, 2)
            sorted_words[GATE, n] = keep.tile([P, HD], BF16, name="gate_wide_%d" % n)
            nc.vector.tensor_tensor(
                out=sorted_words[GATE, n][:].rearrange("p (u q e) -> p u q e", u=2, e=2),
                in0=gate_bytes[a][:, HD * j : HD * (j + 1)].bitcast(FP8).rearrange("p (q u e) -> p u q e", u=2, e=2),
                in1=scale_rows[:].rearrange("p (u q e) -> p u q e", u=2, e=2),
                op=ALU.mult,
            )

        def sort_dw(n):
            a, j = divmod(n, 2)
            sorted_words[DW, n] = keep.tile([P, HD], BF16, name="dw_sorted_%d" % n)
            nc.vector.tensor_copy(
                out=sorted_words[DW, n][:].bitcast(F32).rearrange("p (u q) -> p u q", u=2),
                in_=dw_sb[a][:, HD * j : HD * (j + 1)].bitcast(F32).rearrange("p (q u) -> p u q", u=2),
            )

        def mx_pass(acc, lhs_key, lhs_cols, rhs_key, rhs_cols, start, stop):
            nc.tensor.matmul_mx(
                out=acc[:, 0:C],
                lhsT=codes[lhs_key][:, lhs_cols].bitcast(FP8X4),
                lhsT_scale=scales[lhs_key][:, lhs_cols],
                rhs=codes[rhs_key][:, rhs_cols].bitcast(FP8X4),
                rhs_scale=scales[rhs_key][:, rhs_cols],
                start=start,
                stop=stop,
            )

        def hidden_tile(i):
            g, t = divmod(i, 4)
            acc = psum.tile([P, BANK], F32, name="bank", tag="bank")
            for c in range(4):
                b, half = divmod(c, 2)
                mx_pass(acc, ("psi", i), slice(P * c, P * (c + 1)), ("r", b), slice(C * half, C * (half + 1)), c == 0, c == 3)
            if t == 0:
                hid_planes[g] = keep.tile([P, 4, C], BF16, name="hid_planes_%d" % g)
            nc.scalar.activation(out=hid_planes[g][:, t, :], in_=acc[:, 0:C], func=ACT.Relu, bias=b1[:, g, t : t + 1])

        def interleave_hidden(g):
            grouped["hid", g] = keep.tile([P, 4 * C], BF16, name="hid_grouped_%d" % g, align_bytes=64)
            nc.vector.tensor_copy(
                out=grouped["hid", g][:].rearrange("p (c t) -> p c t", t=4),
                in_=hid_planes[g][:].rearrange("p t c -> p c t"),
            )

        def second_pass(n, which, g):
            if g == 0:
                accs[which, n] = psum.tile([P, BANK], F32, name="bank", tag="bank")
            mx_pass(accs[which, n], (which, n), slice(P * g, P * (g + 1)), ("hid", g), slice(0, C), g == 0, g == 1)

        def gate_product(n):
            a, j = divmod(n, 2)
            gate = ring.tile([P, C], F32, name="gate", tag="gate")
            nc.scalar.activation(
                out=gate[:], in_=accs[GATE, n][:, 0:C], func=ACT.Sigmoid, bias=bias[GATE][:, a, j : j + 1]
            )
            prod[n] = keep.tile([P, C], F32, name="prod_%d" % n)
            nc.vector.scalar_tensor_tensor(
                out=prod[n][:], in0=accs[DW, n][:, 0:C], scalar=bias[DW][:, a, j : j + 1], in1=gate[:],
                op0=ALU.add, op1=ALU.mult,
            )

        def out_tile(n):
            for which in (GATE, DW):
                for g in range(2):
                    second_pass(n, which, g)
            gate_product(n)

        def turn_pair(a):
            bank = psum.tile([P, BANK], F32, name="bank", tag="bank")
            for j in range(2):
                for h in range(2):
                    nc.tensor.transpose(
                        bank[:, P * (2 * h + j) : P * (2 * h + j + 1)],
                        prod[2 * a + j][:, P * h : P * (h + 1)],
                        ident[:],
                    )
            return bank

        def store_pair(a, bank):
            e_cols = slice(256 * a, 256 * (a + 1))
            for h in range(2):
                result = ring.tile([P, 256], F32, name="result", tag="result")
                nc.vector.tensor_tensor(
                    out=result[:].rearrange("c (p j) -> c p j", j=2),
                    in0=bank[:, 256 * h : 256 * (h + 1)].rearrange("c (j p) -> c p j", j=2),
                    in1=w0_rows[:, e_cols].rearrange("c (p j) -> c p j", j=2),
                    op=ALU.add,
                )
                nc.sync.dma_start(out=out[P * h : P * (h + 1), e_cols], in_=result[:])

        spread_scale(0)
        turn_r(0)
        quantize(("r", 0))
        turn_r(1)
        spread_scale(1)
        quantize(("r", 1))
        turn_psi(0)
        quantize(("psi", 0))
        turn_psi(1)
        widen_gate(0)
        for i in range(2, HID_TILES):
            turn_psi(i)
            if i == 2:
                nc.scalar.copy(out=b1[:], in_=b1_raw[:])
            quantize(("psi", i - 1))
            hidden_tile(i - 2)
            if i < 6:
                widen_gate(i - 1)
            if i == 6:
                interleave_hidden(0)
                sort_dw(0)
                quantize(("hid", 0))
            if i == 7:
                sort_dw(1)
                widen_gate(5)
        turn_weights(0)
        quantize(("psi", 7))
        hidden_tile(6)
        quantize_weights(0)
        turn_weights(1)
        quantize_weights(1)
        hidden_tile(7)
        interleave_hidden(1)
        quantize(("hid", 1))
        for g in range(2):
            turn_weights(2 + g)
            quantize_weights(2 + g)
            for n in range(2):
                for which in (GATE, DW):
                    second_pass(n, which, g)
            if g == 0:
                for which in (DW, GATE):
                    bias[which] = keep.tile([P, OUT_PAIRS, 2], F32, name="bias_%d" % which)
                    nc.scalar.copy(out=bias[which][:], in_=bias_raw[which][:])
                sort_dw(4)
                sort_dw(5)
        gate_product(0)
        gate_product(1)
        turn_weights(4)
        turn_weights(5)
        first_pair = turn_pair(0)
        quantize_weights(4)
        store_pair(0, first_pair)
        quantize_weights(5)
        for n in range(2, OUT_TILES):
            out_tile(n)
        for a in range(1, OUT_PAIRS):
            store_pair(a, turn_pair(a))
